import numpy as np
import ml_dtypes


def mxq(x, axis, fmt="e4m3"):
    dtype, down = {"e4m3": (ml_dtypes.float8_e4m3fn, 7), "e5m2": (ml_dtypes.float8_e5m2, 14)}[fmt]
    v = np.moveaxis(np.asarray(x, np.float32).astype(ml_dtypes.bfloat16).astype(np.float64), axis, -1)
    blocks = v.reshape(v.shape[:-1] + (-1, 32))
    amax = np.abs(blocks).max(-1, keepdims=True)
    byte = np.maximum(np.where(amax > 0, np.frexp(amax)[1] - 1 + 127, 0) - down, 1)
    scale = np.exp2(byte - 127.0)
    codes = (blocks / scale).astype(np.float32).astype(dtype).astype(np.float64)
    return np.moveaxis((codes * scale).reshape(v.shape), -1, axis)


WIDE = False


def mx_kscale(k):
    if not WIDE:
        return np.ones(k)
    levels = np.array([10, -10, 5, -5, 0])
    a = np.random.permutation(np.resize(levels, k // 512 * 4)).reshape(k // 512, 4)
    idx = np.arange(k)
    return np.exp2(a[idx // 512, idx % 128 // 32])


BF16 = ml_dtypes.bfloat16


def bf(x):
    return np.asarray(x, np.float32).astype(BF16)


def f64(x):
    return np.asarray(x).astype(np.float64)


N, D, H, HD = 4096, 512, 8, 64
P = H * HD
HALF = HD // 2
EPS = 1e-6


def rms_norm(y):
    ms = np.mean(y * y, axis=-1, keepdims=True) + EPS
    return y * (1.0 / np.sqrt(ms))


def rotate_half(z):
    h = z.shape[-1] // 2
    return np.concatenate([-z[..., h:], z[..., :h]], axis=-1)


def rope_2d(y, cos, sin):
    def ap(z, c, s):
        return z * c[:, None, :] + rotate_half(z) * s[:, None, :]

    return np.concatenate([ap(y[..., :HALF], cos[:, :HALF], sin[:, :HALF]), ap(y[..., HALF:], cos[:, HALF:], sin[:, HALF:])], axis=-1)


def setup_inputs():
    s = mx_kscale(D)
    return {
        "hidden_states": bf(np.random.standard_normal((N, D)) * s),
        "cos": bf(np.random.uniform(-1.0, 1.0, (N, HD))),
        "sin": bf(np.random.uniform(-1.0, 1.0, (N, HD))),
        "Wq": bf(np.random.standard_normal((D, P)) / np.sqrt(D) / s[:, None]),
        "Wk": bf(np.random.standard_normal((D, P)) / np.sqrt(D) / s[:, None]),
        "Wv": bf(np.random.standard_normal((D, P)) / np.sqrt(D) / s[:, None]),
        "q_scale": bf(1.0 + 0.1 * np.random.standard_normal(HD)),
        "k_scale": bf(1.0 + 0.1 * np.random.standard_normal(HD)),
    }


def reference(hidden_states, cos, sin, Wq, Wk, Wv, q_scale, k_scale):
    x = mxq(f64(hidden_states), 1, "e4m3")
    c, s = f64(cos), f64(sin)
    yq = (x @ mxq(f64(Wq), 0, "e4m3")).reshape(N, H, HD)
    yk = (x @ mxq(f64(Wk), 0, "e4m3")).reshape(N, H, HD)
    yv = (x @ mxq(f64(Wv), 0, "e4m3")).reshape(N, H, HD)
    q = rms_norm(yq) * f64(q_scale)
    k = rms_norm(yk) * f64(k_scale)
    v = rms_norm(yv)
    return rope_2d(q, c, s), rope_2d(k, c, s), v

@@ -1,0 +1,233 @@
+from contextlib import ExitStack
+
+import concourse.mybir as mybir
+from concourse.masks import make_identity
+
+F32 = mybir.dt.float32
+BF16 = mybir.dt.bfloat16
+U32 = mybir.dt.uint32
+U8 = mybir.dt.uint8
+FP8X4 = mybir.dt.float8_e4m3fn_x4
+ALU = mybir.AluOpType
+ACT = mybir.ActivationFunctionType
+
+N, D, H, HD = 4096, 512, 8, 64
+P = 128
+NT = N // P
+CH = 4
+NCH = NT // CH
+EPS = 1e-6
+FLOPS = 2 * N * D * 3 * H * HD
+
+
+def tile_torchgemma4visionattention_pa_t_kernel(
+    tc, hidden_states, cos, sin, Wq, Wk, Wv, q_scale, k_scale, out_0, out_1, out_2
+):
+    nc = tc.nc
+    with ExitStack() as ctx:
+        ctx.enter_context(tc.manual_schedule())
+        const = ctx.enter_context(tc.tile_pool(name="const", bufs=1))
+        xin = ctx.enter_context(tc.tile_pool(name="xin", bufs=NCH))
+        xq = ctx.enter_context(tc.tile_pool(name="xq", bufs=2))
+        small = ctx.enter_context(tc.tile_pool(name="small", bufs=4))
+        work = ctx.enter_context(tc.tile_pool(name="work", bufs=3))
+        ps_t = ctx.enter_context(tc.psum_pool(name="ps_t", bufs=2))
+        ps_m = ctx.enter_context(tc.psum_pool(name="ps_m", bufs=2))
+
+        x_v = hidden_states.rearrange("(p t) d -> p t d", t=NT)
+        cos_v = cos.rearrange("(p t) f -> p t f", t=NT)
+        sin_v = sin.rearrange("(p t) f -> p t f", t=NT)
+        out_v = [o.rearrange("(p t) h f -> p t (h f)", t=NT) for o in (out_0, out_1, out_2)]
+
+        raw = []
+        xc = []
+
+        def load_w(w, nm):
+            r = const.tile([P, 4, D], BF16, name="raw_" + nm)
+            nc.sync.dma_start(
+                out=r[:].rearrange("q (u e) c -> q u e c", u=2),
+                in_=w.rearrange("(u q e) c -> q u e c", u=2, e=2),
+            )
+            raw.append(r)
+
+        def load_x(c):
+            t = xin.tile([P, CH, D], BF16, name="xc")
+            nc.sync.dma_start(out=t[:], in_=x_v[:, c * CH : (c + 1) * CH, :])
+            xc.append(t)
+
+        gains = const.tile([P, 2, HD], BF16, name="gains")
+        cos_sb = const.tile([P, NT, HD], BF16, name="cos_sb")
+        sin_sb = const.tile([P, NT, HD], BF16, name="sin_sb")
+        load_x(0)
+        load_w(Wq, "q")
+        nc.sync.dma_start(out=gains[:, 0, :], in_=q_scale.partition_broadcast(P))
+        nc.sync.dma_start(out=gains[:, 1, :], in_=k_scale.partition_broadcast(P))
+        nc.sync.dma_start(out=cos_sb[:, 0:CH, :], in_=cos_v[:, 0:CH, :])
+        nc.sync.dma_start(out=sin_sb[:, 0:CH, :], in_=sin_v[:, 0:CH, :])
+        load_w(Wk, "k")
+        load_w(Wv, "v")
+        nc.sync.dma_start(out=cos_sb[:, CH:NT, :], in_=cos_v[:, CH:NT, :])
+        nc.sync.dma_start(out=sin_sb[:, CH:NT, :], in_=sin_v[:, CH:NT, :])
+        for c in range(1, NCH):
+            load_x(c)
+
+        ident = const.tile([P, P], F32, name="ident")
+        make_identity(nc, ident[:])
+        eps_t = const.tile([P, 1], F32, name="eps_t")
+        nc.vector.memset(eps_t[:], EPS)
+
+        wc = const.tile([P, 3 * 512], U32, name="wc", align_bytes=64)
+        ws = const.tile([P, 3 * 512], U8, name="ws", align_bytes=64)
+        wg = [const.tile([P, 512, 4], BF16, name="wg%d" % i, align_bytes=64) for i in range(3)]
+
+        def regroup_w(i, eng_copy):
+            eng_copy(
+                out=wg[i][:].rearrange("p (c i) t -> p c t i", i=4),
+                in_=raw[i][:].rearrange("p t (c i) -> p c t i", i=4),
+            )
+
+        def quant_w(i):
+            nc.vector.quantize_mx(
+                out=wc[:, i * 512 : (i + 1) * 512].bitcast(FP8X4),
+                scales=ws[:, i * 512 : (i + 1) * 512],
+                in_=wg[i][:].rearrange("p c t -> p (c t)"),
+            )
+
+        sinsw = const.tile([P, NT, HD], BF16, name="sinsw")
+        tab = const.tile([P, NT, 2, 2, HD], F32, name="tab")
+
+        def swap_sin(c):
+            ts = slice(c * CH, (c + 1) * CH)
+            sn = sin_sb[:, ts, :].rearrange("p t (b s i) -> p (t b) s i", b=2, s=2)
+            sw = sinsw[:, ts, :].rearrange("p t (b s i) -> p (t b) s i", b=2, s=2)
+            nc.vector.tensor_copy(out=sw[:, :, 0, :], in_=sn[:, :, 1, :])
+            nc.vector.tensor_scalar(out=sw[:, :, 1, :], in0=sn[:, :, 0, :], scalar1=-1.0, scalar2=None, op0=ALU.mult)
+
+        def build_tab(c, two):
+            ts = slice(c * CH, (c + 1) * CH)
+            src = cos_sb if two == 0 else sinsw
+            nc.gpsimd.tensor_tensor(
+                out=tab[:, ts, :, two, :],
+                in0=src[:, ts, :].unsqueeze(2).to_broadcast([P, CH, 2, HD]),
+                in1=gains[:].unsqueeze(1).to_broadcast([P, CH, 2, HD]),
+                op=ALU.mult,
+            )
+
+        xg_of = {}
+        xcodes = {}
+
+        def x_transpose(c, half):
+            xw = xc[c][:].bitcast(F32)
+            xt = ps_t.tile([P, 512], F32, name="xt")
+            for a in range(2):
+                for u in range(2):
+                    nc.tensor.transpose(
+                        xt[:, (a * 2 + u) * P : (a * 2 + u + 1) * P],
+                        xw[:, half * 2 + a, u * P : (u + 1) * P],
+                        ident[:],
+                    )
+            return xt
+
+        def x_copy(c, half, xt):
+            if half == 0:
+                xg_of[c] = xq.tile([P, CH, P, 4], BF16, name="xg", align_bytes=64)
+            xgw = xg_of[c][:].rearrange("p a k t -> p a (k t)").bitcast(F32).rearrange("p a (k u) -> p a k u", u=2)
+            nc.scalar.copy(
+                out=xgw[:, half * 2 : half * 2 + 2],
+                in_=xt[:].rearrange("p (a u k) -> p a k u", a=2, u=2),
+            )
+
+        def x_quant(c):
+            xcod = xq.tile([P, CH * P], U32, name="xcod", align_bytes=64)
+            xsc = xq.tile([P, CH * P], U8, name="xsc", align_bytes=64)
+            nc.vector.quantize_mx(
+                out=xcod[:].bitcast(FP8X4),
+                scales=xsc[:],
+                in_=xg_of[c][:].rearrange("p a k t -> p (a k t)"),
+            )
+            xcodes[c] = (xcod, xsc)
+
+        xt0 = x_transpose(0, 0)
+        xt1 = x_transpose(0, 1)
+        x_copy(0, 0, xt0)
+        x_copy(0, 1, xt1)
+        regroup_w(0, nc.vector.tensor_copy)
+        regroup_w(1, nc.scalar.copy)
+        x_quant(0)
+        quant_w(0)
+        swap_sin(0)
+        regroup_w(2, nc.vector.tensor_copy)
+        quant_w(1)
+        quant_w(2)
+        build_tab(0, 0)
+        build_tab(0, 1)
+
+        for t in range(NT):
+            c, a = divmod(t, CH)
+            more = c + 1 < NCH
+            xcod, xsc = xcodes[c]
+            acc = []
+            for i in range(3):
+                b = ps_m.tile([P, H, HD], F32, name="acc%d" % i)
+                nc.tensor.matmul_mx(
+                    out=b[:].rearrange("p h f -> p (h f)"),
+                    lhsT=xcod[:, a * P : (a + 1) * P].bitcast(FP8X4),
+                    lhsT_scale=xsc[:, a * P : (a + 1) * P],
+                    rhs=wc[:, i * 512 : (i + 1) * 512].bitcast(FP8X4),
+                    rhs_scale=ws[:, i * 512 : (i + 1) * 512],
+                    start=True,
+                    stop=True,
+                )
+                acc.append(b)
+            xt = x_transpose(c + 1, a) if more and a < 2 else None
+
+            ss = small.tile([P, 3 * H], F32, name="ss")
+            for i in range(3):
+                for h in range(H):
+                    junk = small.tile([P, HD], BF16, name="junk")
+                    nc.scalar.activation(
+                        out=junk[:], in_=acc[i][:, h, :], func=ACT.Square, accum_out=ss[:, i * H + h : i * H + h + 1]
+                    )
+            rt = small.tile([P, 3 * H], F32, name="rt")
+            nc.scalar.activation(out=rt[:], in_=ss[:], func=ACT.Sqrt, bias=eps_t[:, 0:1], scale=1.0 / HD)
+            if xt is not None:
+                x_copy(c + 1, a, xt)
+
+            if more and a == 0:
+                swap_sin(c + 1)
+            if more and a == 2:
+                x_quant(c + 1)
+            rstd = small.tile([P, 3 * H], F32, name="rstd")
+            nc.vector.reciprocal(out=rstd[:], in_=rt[:])
+            uw = work.tile([P, 2, 2, H * HD], F32, name="uw")
+            for k in range(2):
+                for h in range(H):
+                    nc.vector.scalar_tensor_tensor(
+                        out=uw[:, k, :, h * HD : (h + 1) * HD],
+                        in0=acc[k][:, h : h + 1, :].to_broadcast([P, 2, HD]),
+                        scalar=rstd[:, k * H + h : k * H + h + 1],
+                        in1=tab[:, t, k, :, :],
+                        op0=ALU.mult,
+                        op1=ALU.mult,
+                    )
+            ov = work.tile([P, H, HD], F32, name="ov")
+            nc.vector.tensor_tensor(
+                out=ov[:],
+                in0=acc[2][:],
+                in1=rstd[:, 2 * H : 3 * H].unsqueeze(2).to_broadcast([P, H, HD]),
+                op=ALU.mult,
+            )
+
+            if more and a < 2:
+                build_tab(c + 1, a)
+            o = work.tile([P, 2, H * HD], F32, name="o")
+            ovw = o[:].rearrange("p k (m s i) -> p k m s i", s=2, i=16)
+            uv = uw[:].rearrange("p k two (m s i) -> p k two m s i", s=2, i=16)
+            for s in range(2):
+                nc.gpsimd.tensor_tensor(
+                    out=ovw[:, :, :, s, :], in0=uv[:, :, 0, :, s, :], in1=uv[:, :, 1, :, 1 - s, :], op=ALU.add
+                )
+
+            nc.sync.dma_start(out=out_v[2][:, t, :], in_=ov[:].rearrange("p h f -> p (h f)"))
+            nc.sync.dma_start(out=out_v[0][:, t, :], in_=o[:, 0, :])
+            nc.sync.dma_start(out=out_v[1][:, t, :], in_=o[:, 1, :])

@@ -14,8 +14,10 @@ ACT = mybir.ActivationFunctionType
 N, D, H, HD = 4096, 512, 8, 64
 P = 128
 NT = N // P
-CH = 4
-NCH = NT // CH
+NP = NT // 2
+TCH = 4
+NTC = NT // TCH
+LAG = 4
 EPS = 1e-6
 FLOPS = 2 * N * D * 3 * H * HD
 
@@ -27,12 +29,13 @@ def tile_torchgemma4visionattention_pa_t_kernel(
     with ExitStack() as ctx:
         ctx.enter_context(tc.manual_schedule())
         const = ctx.enter_context(tc.tile_pool(name="const", bufs=1))
-        xin = ctx.enter_context(tc.tile_pool(name="xin", bufs=NCH))
-        xq = ctx.enter_context(tc.tile_pool(name="xq", bufs=2))
+        xin = ctx.enter_context(tc.tile_pool(name="xin", bufs=NP))
+        xgp = ctx.enter_context(tc.tile_pool(name="xgp", bufs=2))
+        xq = ctx.enter_context(tc.tile_pool(name="xq", bufs=4))
         small = ctx.enter_context(tc.tile_pool(name="small", bufs=4))
-        work = ctx.enter_context(tc.tile_pool(name="work", bufs=3))
-        ps_t = ctx.enter_context(tc.psum_pool(name="ps_t", bufs=2))
-        ps_m = ctx.enter_context(tc.psum_pool(name="ps_m", bufs=2))
+        work = ctx.enter_context(tc.tile_pool(name="work", bufs=4))
+        ps_t = ctx.enter_context(tc.psum_pool(name="ps_t", bufs=1))
+        ps_m = ctx.enter_context(tc.psum_pool(name="ps_m", bufs=7))
 
         x_v = hidden_states.rearrange("(p t) d -> p t d", t=NT)
         cos_v = cos.rearrange("(p t) f -> p t f", t=NT)
@@ -50,9 +53,9 @@ def tile_torchgemma4visionattention_pa_t_kernel(
             )
             raw.append(r)
 
-        def load_x(c):
-            t = xin.tile([P, CH, D], BF16, name="xc")
-            nc.sync.dma_start(out=t[:], in_=x_v[:, c * CH : (c + 1) * CH, :])
+        def load_x(pr):
+            t = xin.tile([P, 2, D], BF16, name="xc")
+            nc.sync.dma_start(out=t[:], in_=x_v[:, 2 * pr : 2 * pr + 2, :])
             xc.append(t)
 
         gains = const.tile([P, 2, HD], BF16, name="gains")
@@ -62,19 +65,22 @@ def tile_torchgemma4visionattention_pa_t_kernel(
         load_w(Wq, "q")
         nc.sync.dma_start(out=gains[:, 0, :], in_=q_scale.partition_broadcast(P))
         nc.sync.dma_start(out=gains[:, 1, :], in_=k_scale.partition_broadcast(P))
-        nc.sync.dma_start(out=cos_sb[:, 0:CH, :], in_=cos_v[:, 0:CH, :])
-        nc.sync.dma_start(out=sin_sb[:, 0:CH, :], in_=sin_v[:, 0:CH, :])
+        nc.sync.dma_start(out=cos_sb[:, 0:TCH, :], in_=cos_v[:, 0:TCH, :])
+        nc.sync.dma_start(out=sin_sb[:, 0:TCH, :], in_=sin_v[:, 0:TCH, :])
         load_w(Wk, "k")
         load_w(Wv, "v")
-        nc.sync.dma_start(out=cos_sb[:, CH:NT, :], in_=cos_v[:, CH:NT, :])
-        nc.sync.dma_start(out=sin_sb[:, CH:NT, :], in_=sin_v[:, CH:NT, :])
-        for c in range(1, NCH):
-            load_x(c)
+        load_x(1)
+        nc.sync.dma_start(out=cos_sb[:, TCH:NT, :], in_=cos_v[:, TCH:NT, :])
+        nc.sync.dma_start(out=sin_sb[:, TCH:NT, :], in_=sin_v[:, TCH:NT, :])
+        for pr in range(2, NP):
+            load_x(pr)
 
         ident = const.tile([P, P], F32, name="ident")
         make_identity(nc, ident[:])
         eps_t = const.tile([P, 1], F32, name="eps_t")
         nc.vector.memset(eps_t[:], EPS)
+        warm = const.tile([P, 1], F32, name="warm")
+        nc.scalar.activation(out=warm[:], in_=eps_t[:], func=ACT.Abs_reciprocal_sqrt)
 
         wc = const.tile([P, 3 * 512], U32, name="wc", align_bytes=64)
         ws = const.tile([P, 3 * 512], U8, name="ws", align_bytes=64)
@@ -97,108 +103,87 @@ def tile_torchgemma4visionattention_pa_t_kernel(
         tab = const.tile([P, NT, 2, 2, HD], F32, name="tab")
 
         def swap_sin(c):
-            ts = slice(c * CH, (c + 1) * CH)
+            ts = slice(c * TCH, (c + 1) * TCH)
             sn = sin_sb[:, ts, :].rearrange("p t (b s i) -> p (t b) s i", b=2, s=2)
             sw = sinsw[:, ts, :].rearrange("p t (b s i) -> p (t b) s i", b=2, s=2)
             nc.vector.tensor_copy(out=sw[:, :, 0, :], in_=sn[:, :, 1, :])
             nc.vector.tensor_scalar(out=sw[:, :, 1, :], in0=sn[:, :, 0, :], scalar1=-1.0, scalar2=None, op0=ALU.mult)
 
         def build_tab(c, two):
-            ts = slice(c * CH, (c + 1) * CH)
+            ts = slice(c * TCH, (c + 1) * TCH)
             src = cos_sb if two == 0 else sinsw
             nc.gpsimd.tensor_tensor(
                 out=tab[:, ts, :, two, :],
-                in0=src[:, ts, :].unsqueeze(2).to_broadcast([P, CH, 2, HD]),
-                in1=gains[:].unsqueeze(1).to_broadcast([P, CH, 2, HD]),
+                in0=src[:, ts, :].unsqueeze(2).to_broadcast([P, TCH, 2, HD]),
+                in1=gains[:].unsqueeze(1).to_broadcast([P, TCH, 2, HD]),
                 op=ALU.mult,
             )
 
-        xg_of = {}
+        xts = {}
+        xgs = {}
         xcodes = {}
 
-        def x_transpose(c, half):
-            xw = xc[c][:].bitcast(F32)
+        def x_transpose(pr):
+            xw = xc[pr][:].bitcast(F32)
             xt = ps_t.tile([P, 512], F32, name="xt")
             for a in range(2):
                 for u in range(2):
                     nc.tensor.transpose(
-                        xt[:, (a * 2 + u) * P : (a * 2 + u + 1) * P],
-                        xw[:, half * 2 + a, u * P : (u + 1) * P],
-                        ident[:],
+                        xt[:, (a * 2 + u) * P : (a * 2 + u + 1) * P], xw[:, a, u * P : (u + 1) * P], ident[:]
                     )
-            return xt
+            xts[pr] = xt
 
-        def x_copy(c, half, xt):
-            if half == 0:
-                xg_of[c] = xq.tile([P, CH, P, 4], BF16, name="xg", align_bytes=64)
-            xgw = xg_of[c][:].rearrange("p a k t -> p a (k t)").bitcast(F32).rearrange("p a (k u) -> p a k u", u=2)
-            nc.scalar.copy(
-                out=xgw[:, half * 2 : half * 2 + 2],
-                in_=xt[:].rearrange("p (a u k) -> p a k u", a=2, u=2),
-            )
+        def x_copy(pr):
+            xg = xgp.tile([P, 2, P, 4], BF16, name="xg", align_bytes=64)
+            xgw = xg[:].rearrange("p a k t -> p a (k t)").bitcast(F32).rearrange("p a (k u) -> p a k u", u=2)
+            nc.scalar.copy(out=xgw, in_=xts[pr][:].rearrange("p (a u k) -> p a k u", a=2, u=2))
+            xgs[pr] = xg
 
-        def x_quant(c):
-            xcod = xq.tile([P, CH * P], U32, name="xcod", align_bytes=64)
-            xsc = xq.tile([P, CH * P], U8, name="xsc", align_bytes=64)
+        def x_quant(pr):
+            xcod = xq.tile([P, 2 * P], U32, name="xcod", align_bytes=64)
+            xsc = xq.tile([P, 2 * P], U8, name="xsc", align_bytes=64)
             nc.vector.quantize_mx(
-                out=xcod[:].bitcast(FP8X4),
-                scales=xsc[:],
-                in_=xg_of[c][:].rearrange("p a k t -> p (a k t)"),
+                out=xcod[:].bitcast(FP8X4), scales=xsc[:], in_=xgs[pr][:].rearrange("p a k t -> p (a k t)")
             )
-            xcodes[c] = (xcod, xsc)
+            xcodes[pr] = (xcod, xsc)
 
-        xt0 = x_transpose(0, 0)
-        xt1 = x_transpose(0, 1)
-        x_copy(0, 0, xt0)
-        x_copy(0, 1, xt1)
+        x_transpose(0)
+        x_copy(0)
+        x_transpose(1)
+        x_copy(1)
         regroup_w(0, nc.vector.tensor_copy)
         regroup_w(1, nc.scalar.copy)
         x_quant(0)
         quant_w(0)
         swap_sin(0)
+        x_quant(1)
         regroup_w(2, nc.vector.tensor_copy)
         quant_w(1)
         quant_w(2)
-        build_tab(0, 0)
-        build_tab(0, 1)
+        swap_sin(1)
+        for c in range(2):
+            for two in range(2):
+                build_tab(c, two)
 
-        for t in range(NT):
-            c, a = divmod(t, CH)
-            more = c + 1 < NCH
-            xcod, xsc = xcodes[c]
-            acc = []
-            for i in range(3):
-                b = ps_m.tile([P, H, HD], F32, name="acc%d" % i)
-                nc.tensor.matmul_mx(
-                    out=b[:].rearrange("p h f -> p (h f)"),
-                    lhsT=xcod[:, a * P : (a + 1) * P].bitcast(FP8X4),
-                    lhsT_scale=xsc[:, a * P : (a + 1) * P],
-                    rhs=wc[:, i * 512 : (i + 1) * 512].bitcast(FP8X4),
-                    rhs_scale=ws[:, i * 512 : (i + 1) * 512],
-                    start=True,
-                    stop=True,
-                )
-                acc.append(b)
-            xt = x_transpose(c + 1, a) if more and a < 2 else None
+        accs = {}
+        sums = {}
+        rstds = {}
 
-            ss = small.tile([P, 3 * H], F32, name="ss")
-            for i in range(3):
-                for h in range(H):
-                    junk = small.tile([P, HD], BF16, name="junk")
-                    nc.scalar.activation(
-                        out=junk[:], in_=acc[i][:, h, :], func=ACT.Square, accum_out=ss[:, i * H + h : i * H + h + 1]
-                    )
-            rt = small.tile([P, 3 * H], F32, name="rt")
-            nc.scalar.activation(out=rt[:], in_=ss[:], func=ACT.Sqrt, bias=eps_t[:, 0:1], scale=1.0 / HD)
-            if xt is not None:
-                x_copy(c + 1, a, xt)
-
-            if more and a == 0:
-                swap_sin(c + 1)
-            if more and a == 2:
-                x_quant(c + 1)
+        def factors(t):
             rstd = small.tile([P, 3 * H], F32, name="rstd")
-            nc.vector.reciprocal(out=rstd[:], in_=rt[:])
+            nc.scalar.activation(
+                out=rstd[:], in_=sums[t][:], func=ACT.Abs_reciprocal_sqrt, bias=eps_t[:, 0:1], scale=1.0 / HD
+            )
+            rstds[t] = rstd
+
+        def finish(t):
+            c, a = divmod(t, TCH)
+            acc = accs[t]
+            rstd = rstds[t]
+            if a == 0 and c + 2 < NTC:
+                swap_sin(c + 2)
+            if t % 2 == 1 and t // 2 + 2 < NP:
+                x_quant(t // 2 + 2)
             uw = work.tile([P, 2, 2, H * HD], F32, name="uw")
             for k in range(2):
                 for h in range(H):
@@ -217,9 +202,8 @@ def tile_torchgemma4visionattention_pa_t_kernel(
                 in1=rstd[:, 2 * H : 3 * H].unsqueeze(2).to_broadcast([P, H, HD]),
                 op=ALU.mult,
             )
-
-            if more and a < 2:
-                build_tab(c + 1, a)
+            if a < 2 and c + 2 < NTC:
+                build_tab(c + 2, a)
             o = work.tile([P, 2, H * HD], F32, name="o")
             ovw = o[:].rearrange("p k (m s i) -> p k m s i", s=2, i=16)
             uv = uw[:].rearrange("p k two (m s i) -> p k two m s i", s=2, i=16)
@@ -227,7 +211,43 @@ def tile_torchgemma4visionattention_pa_t_kernel(
                 nc.gpsimd.tensor_tensor(
                     out=ovw[:, :, :, s, :], in0=uv[:, :, 0, :, s, :], in1=uv[:, :, 1, :, 1 - s, :], op=ALU.add
                 )
-
             nc.sync.dma_start(out=out_v[2][:, t, :], in_=ov[:].rearrange("p h f -> p (h f)"))
             nc.sync.dma_start(out=out_v[0][:, t, :], in_=o[:, 0, :])
             nc.sync.dma_start(out=out_v[1][:, t, :], in_=o[:, 1, :])
+
+        for t in range(NT):
+            pr, a = divmod(t, 2)
+            ahead = a == 0 and pr + 2 < NP
+            xcod, xsc = xcodes[pr]
+            acc = []
+            for i in range(3):
+                b = ps_m.tile([P, H, HD], F32, name="acc")
+                nc.tensor.matmul_mx(
+                    out=b[:].rearrange("p h f -> p (h f)"),
+                    lhsT=xcod[:, a * P : (a + 1) * P].bitcast(FP8X4),
+                    lhsT_scale=xsc[:, a * P : (a + 1) * P],
+                    rhs=wc[:, i * 512 : (i + 1) * 512].bitcast(FP8X4),
+                    rhs_scale=ws[:, i * 512 : (i + 1) * 512],
+                    start=True,
+                    stop=True,
+                )
+                acc.append(b)
+            accs[t] = acc
+            if ahead:
+                x_transpose(pr + 2)
+
+            ss = small.tile([P, 3 * H], F32, name="ss")
+            sums[t] = ss
+            for j in range(3 * H):
+                junk = small.tile([P, HD], BF16, name="junk")
+                nc.scalar.activation(
+                    out=junk[:], in_=acc[j // H][:, j % H, :], func=ACT.Square, accum_out=ss[:, j : j + 1]
+                )
+                if j == LAG - 1 and t > 0:
+                    factors(t - 1)
+            if ahead:
+                x_copy(pr + 2)
+            if t > 0:
+                finish(t - 1)
+        factors(NT - 1)
+        finish(NT - 1)

@@ -63,15 +63,15 @@ def tile_torchgemma4visionattention_pa_t_kernel(
         sin_sb = const.tile([P, NT, HD], BF16, name="sin_sb")
         load_x(0)
         load_w(Wq, "q")
+        load_w(Wk, "k")
+        load_w(Wv, "v")
         nc.sync.dma_start(out=gains[:, 0, :], in_=q_scale.partition_broadcast(P))
         nc.sync.dma_start(out=gains[:, 1, :], in_=k_scale.partition_broadcast(P))
         nc.sync.dma_start(out=cos_sb[:, 0:TCH, :], in_=cos_v[:, 0:TCH, :])
         nc.sync.dma_start(out=sin_sb[:, 0:TCH, :], in_=sin_v[:, 0:TCH, :])
-        load_w(Wk, "k")
-        load_w(Wv, "v")
         load_x(1)
-        nc.sync.dma_start(out=cos_sb[:, TCH:NT, :], in_=cos_v[:, TCH:NT, :])
         nc.sync.dma_start(out=sin_sb[:, TCH:NT, :], in_=sin_v[:, TCH:NT, :])
+        nc.sync.dma_start(out=cos_sb[:, TCH:NT, :], in_=cos_v[:, TCH:NT, :])
         for pr in range(2, NP):
             load_x(pr)
 
@@ -102,8 +102,8 @@ def tile_torchgemma4visionattention_pa_t_kernel(
         sinsw = const.tile([P, NT, HD], BF16, name="sinsw")
         tab = const.tile([P, NT, 2, 2, HD], F32, name="tab")
 
-        def swap_sin(c):
-            ts = slice(c * TCH, (c + 1) * TCH)
+        def swap_sin(t0, t1):
+            ts = slice(t0, t1)
             sn = sin_sb[:, ts, :].rearrange("p t (b s i) -> p (t b) s i", b=2, s=2)
             sw = sinsw[:, ts, :].rearrange("p t (b s i) -> p (t b) s i", b=2, s=2)
             nc.vector.tensor_copy(out=sw[:, :, 0, :], in_=sn[:, :, 1, :])
@@ -133,10 +133,10 @@ def tile_torchgemma4visionattention_pa_t_kernel(
                     )
             xts[pr] = xt
 
-        def x_copy(pr):
+        def x_copy(pr, eng_copy):
             xg = xgp.tile([P, 2, P, 4], BF16, name="xg", align_bytes=64)
             xgw = xg[:].rearrange("p a k t -> p a (k t)").bitcast(F32).rearrange("p a (k u) -> p a k u", u=2)
-            nc.scalar.copy(out=xgw, in_=xts[pr][:].rearrange("p (a u k) -> p a k u", a=2, u=2))
+            eng_copy(out=xgw, in_=xts[pr][:].rearrange("p (a u k) -> p a k u", a=2, u=2))
             xgs[pr] = xg
 
         def x_quant(pr):
@@ -148,22 +148,15 @@ def tile_torchgemma4visionattention_pa_t_kernel(
             xcodes[pr] = (xcod, xsc)
 
         x_transpose(0)
-        x_copy(0)
-        x_transpose(1)
-        x_copy(1)
+        x_copy(0, nc.scalar.copy)
         regroup_w(0, nc.vector.tensor_copy)
         regroup_w(1, nc.scalar.copy)
         x_quant(0)
         quant_w(0)
-        swap_sin(0)
-        x_quant(1)
         regroup_w(2, nc.vector.tensor_copy)
         quant_w(1)
         quant_w(2)
-        swap_sin(1)
-        for c in range(2):
-            for two in range(2):
-                build_tab(c, two)
+        swap_sin(0, TCH)
 
         accs = {}
         sums = {}
@@ -180,10 +173,10 @@ def tile_torchgemma4visionattention_pa_t_kernel(
             c, a = divmod(t, TCH)
             acc = accs[t]
             rstd = rstds[t]
-            if a == 0 and c + 2 < NTC:
-                swap_sin(c + 2)
-            if t % 2 == 1 and t // 2 + 2 < NP:
-                x_quant(t // 2 + 2)
+            if t % 2 == 1 and (t + 3) // 2 < NP:
+                x_copy((t + 3) // 2, nc.vector.tensor_copy)
+            if t % 2 == 0 and t >= 2 and (t + 2) // 2 < NP:
+                x_quant((t + 2) // 2)
             uw = work.tile([P, 2, 2, H * HD], F32, name="uw")
             for k in range(2):
                 for h in range(H):
@@ -207,8 +200,9 @@ def tile_torchgemma4visionattention_pa_t_kernel(
             o = work.tile([P, 2, H * HD], F32, name="o")
             ovw = o[:].rearrange("p k (m s i) -> p k m s i", s=2, i=16)
             uv = uw[:].rearrange("p k two (m s i) -> p k two m s i", s=2, i=16)
+            adder = nc.vector if t == NT - 1 else nc.gpsimd
             for s in range(2):
-                nc.gpsimd.tensor_tensor(
+                adder.tensor_tensor(
                     out=ovw[:, :, :, s, :], in0=uv[:, :, 0, :, s, :], in1=uv[:, :, 1, :, 1 - s, :], op=ALU.add
                 )
             nc.sync.dma_start(out=out_v[2][:, t, :], in_=ov[:].rearrange("p h f -> p (h f)"))
@@ -217,7 +211,6 @@ def tile_torchgemma4visionattention_pa_t_kernel(
 
         for t in range(NT):
             pr, a = divmod(t, 2)
-            ahead = a == 0 and pr + 2 < NP
             xcod, xsc = xcodes[pr]
             acc = []
             for i in range(3):
@@ -233,8 +226,16 @@ def tile_torchgemma4visionattention_pa_t_kernel(
                 )
                 acc.append(b)
             accs[t] = acc
-            if ahead:
-                x_transpose(pr + 2)
+            if t == 0:
+                x_transpose(1)
+                x_copy(1, nc.vector.tensor_copy)
+                swap_sin(TCH, NT)
+                x_quant(1)
+                for c in range(2):
+                    for two in range(2):
+                        build_tab(c, two)
+            if a == 1 and (t + 3) // 2 < NP:
+                x_transpose((t + 3) // 2)
 
             ss = small.tile([P, 3 * H], F32, name="ss")
             sums[t] = ss
@@ -245,8 +246,6 @@ def tile_torchgemma4visionattention_pa_t_kernel(
                 )
                 if j == LAG - 1 and t > 0:
                     factors(t - 1)
-            if ahead:
-                x_copy(pr + 2)
             if t > 0:
                 finish(t - 1)
         factors(NT - 1)

@@ -13,11 +13,13 @@ ACT = mybir.ActivationFunctionType
 
 N, D, H, HD = 4096, 512, 8, 64
 P = 128
+PACK = 4
 NT = N // P
-NP = NT // 2
-TCH = 4
-NTC = NT // TCH
+NPAIR = NT // 2
+TAB = 4
+NTAB = NT // TAB
 LAG = 4
+RING = 7
 EPS = 1e-6
 FLOPS = 2 * N * D * 3 * H * HD
 
@@ -29,34 +31,34 @@ def tile_torchgemma4visionattention_pa_t_kernel(
     with ExitStack() as ctx:
         ctx.enter_context(tc.manual_schedule())
         const = ctx.enter_context(tc.tile_pool(name="const", bufs=1))
-        xin = ctx.enter_context(tc.tile_pool(name="xin", bufs=NP))
-        xgp = ctx.enter_context(tc.tile_pool(name="xgp", bufs=2))
-        xq = ctx.enter_context(tc.tile_pool(name="xq", bufs=4))
+        x_in = ctx.enter_context(tc.tile_pool(name="x_in", bufs=NPAIR))
+        x_grouped = ctx.enter_context(tc.tile_pool(name="x_grouped", bufs=2))
+        x_mx = ctx.enter_context(tc.tile_pool(name="x_mx", bufs=4))
         small = ctx.enter_context(tc.tile_pool(name="small", bufs=4))
         work = ctx.enter_context(tc.tile_pool(name="work", bufs=4))
-        ps_t = ctx.enter_context(tc.psum_pool(name="ps_t", bufs=1))
-        ps_m = ctx.enter_context(tc.psum_pool(name="ps_m", bufs=7))
+        psum_t = ctx.enter_context(tc.psum_pool(name="psum_t", bufs=1))
+        psum_y = ctx.enter_context(tc.psum_pool(name="psum_y", bufs=RING))
 
-        x_v = hidden_states.rearrange("(p t) d -> p t d", t=NT)
-        cos_v = cos.rearrange("(p t) f -> p t f", t=NT)
-        sin_v = sin.rearrange("(p t) f -> p t f", t=NT)
-        out_v = [o.rearrange("(p t) h f -> p t (h f)", t=NT) for o in (out_0, out_1, out_2)]
+        x_view = hidden_states.rearrange("(p t) d -> p t d", t=NT)
+        cos_view = cos.rearrange("(p t) f -> p t f", t=NT)
+        sin_view = sin.rearrange("(p t) f -> p t f", t=NT)
+        out_views = [o.rearrange("(p t) h f -> p t (h f)", t=NT) for o in (out_0, out_1, out_2)]
 
-        raw = []
-        xc = []
+        w_raw = []
+        x_raw = []
 
-        def load_w(w, nm):
-            r = const.tile([P, 4, D], BF16, name="raw_" + nm)
+        def load_w(w, label):
+            raw = const.tile([P, PACK, D], BF16, name="w_raw_" + label)
             nc.sync.dma_start(
-                out=r[:].rearrange("q (u e) c -> q u e c", u=2),
-                in_=w.rearrange("(u q e) c -> q u e c", u=2, e=2),
+                out=raw[:].rearrange("p (u e) c -> p u e c", u=2),
+                in_=w.rearrange("(u p e) c -> p u e c", u=2, e=2),
             )
-            raw.append(r)
+            w_raw.append(raw)
 
-        def load_x(pr):
-            t = xin.tile([P, 2, D], BF16, name="xc")
-            nc.sync.dma_start(out=t[:], in_=x_v[:, 2 * pr : 2 * pr + 2, :])
-            xc.append(t)
+        def load_x(pair):
+            raw = x_in.tile([P, 2, D], BF16, name="x_raw")
+            nc.sync.dma_start(out=raw[:], in_=x_view[:, 2 * pair : 2 * pair + 2, :])
+            x_raw.append(raw)
 
         gains = const.tile([P, 2, HD], BF16, name="gains")
         cos_sb = const.tile([P, NT, HD], BF16, name="cos_sb")
@@ -67,186 +69,196 @@ def tile_torchgemma4visionattention_pa_t_kernel(
         load_w(Wv, "v")
         nc.sync.dma_start(out=gains[:, 0, :], in_=q_scale.partition_broadcast(P))
         nc.sync.dma_start(out=gains[:, 1, :], in_=k_scale.partition_broadcast(P))
-        nc.sync.dma_start(out=cos_sb[:, 0:TCH, :], in_=cos_v[:, 0:TCH, :])
-        nc.sync.dma_start(out=sin_sb[:, 0:TCH, :], in_=sin_v[:, 0:TCH, :])
+        nc.sync.dma_start(out=cos_sb[:, 0:TAB, :], in_=cos_view[:, 0:TAB, :])
+        nc.sync.dma_start(out=sin_sb[:, 0:TAB, :], in_=sin_view[:, 0:TAB, :])
         load_x(1)
-        nc.sync.dma_start(out=sin_sb[:, TCH:NT, :], in_=sin_v[:, TCH:NT, :])
-        nc.sync.dma_start(out=cos_sb[:, TCH:NT, :], in_=cos_v[:, TCH:NT, :])
-        for pr in range(2, NP):
-            load_x(pr)
+        nc.sync.dma_start(out=sin_sb[:, TAB:NT, :], in_=sin_view[:, TAB:NT, :])
+        nc.sync.dma_start(out=cos_sb[:, TAB:NT, :], in_=cos_view[:, TAB:NT, :])
+        for pair in range(2, NPAIR):
+            load_x(pair)
 
-        ident = const.tile([P, P], F32, name="ident")
-        make_identity(nc, ident[:])
-        eps_t = const.tile([P, 1], F32, name="eps_t")
-        nc.vector.memset(eps_t[:], EPS)
+        identity = const.tile([P, P], F32, name="identity")
+        make_identity(nc, identity[:])
+        eps_tile = const.tile([P, 1], F32, name="eps_tile")
+        nc.vector.memset(eps_tile[:], EPS)
         warm = const.tile([P, 1], F32, name="warm")
-        nc.scalar.activation(out=warm[:], in_=eps_t[:], func=ACT.Abs_reciprocal_sqrt)
+        nc.scalar.activation(out=warm[:], in_=eps_tile[:], func=ACT.Abs_reciprocal_sqrt)
 
-        wc = const.tile([P, 3 * 512], U32, name="wc", align_bytes=64)
-        ws = const.tile([P, 3 * 512], U8, name="ws", align_bytes=64)
-        wg = [const.tile([P, 512, 4], BF16, name="wg%d" % i, align_bytes=64) for i in range(3)]
+        w_codes = const.tile([P, 3 * D], U32, name="w_codes", align_bytes=64)
+        w_scales = const.tile([P, 3 * D], U8, name="w_scales", align_bytes=64)
+        w_grouped = [const.tile([P, D, PACK], BF16, name="w_grouped%d" % i, align_bytes=64) for i in range(3)]
 
-        def regroup_w(i, eng_copy):
-            eng_copy(
-                out=wg[i][:].rearrange("p (c i) t -> p c t i", i=4),
-                in_=raw[i][:].rearrange("p t (c i) -> p c t i", i=4),
+        def regroup_w(i, copy):
+            copy(
+                out=w_grouped[i][:].rearrange("p (c i) t -> p c t i", i=4),
+                in_=w_raw[i][:].rearrange("p t (c i) -> p c t i", i=4),
             )
 
-        def quant_w(i):
+        def quantise_w(i):
             nc.vector.quantize_mx(
-                out=wc[:, i * 512 : (i + 1) * 512].bitcast(FP8X4),
-                scales=ws[:, i * 512 : (i + 1) * 512],
-                in_=wg[i][:].rearrange("p c t -> p (c t)"),
+                out=w_codes[:, i * D : (i + 1) * D].bitcast(FP8X4),
+                scales=w_scales[:, i * D : (i + 1) * D],
+                in_=w_grouped[i][:].rearrange("p c t -> p (c t)"),
             )
 
-        sinsw = const.tile([P, NT, HD], BF16, name="sinsw")
-        tab = const.tile([P, NT, 2, 2, HD], F32, name="tab")
+        sin_swapped = const.tile([P, NT, HD], BF16, name="sin_swapped")
+        table = const.tile([P, NT, 2, 2, HD], F32, name="table")
 
         def swap_sin(t0, t1):
-            ts = slice(t0, t1)
-            sn = sin_sb[:, ts, :].rearrange("p t (b s i) -> p (t b) s i", b=2, s=2)
-            sw = sinsw[:, ts, :].rearrange("p t (b s i) -> p (t b) s i", b=2, s=2)
-            nc.vector.tensor_copy(out=sw[:, :, 0, :], in_=sn[:, :, 1, :])
-            nc.vector.tensor_scalar(out=sw[:, :, 1, :], in0=sn[:, :, 0, :], scalar1=-1.0, scalar2=None, op0=ALU.mult)
+            plain = sin_sb[:, t0:t1, :].rearrange("p t (b s i) -> p (t b) s i", b=2, s=2)
+            swapped = sin_swapped[:, t0:t1, :].rearrange("p t (b s i) -> p (t b) s i", b=2, s=2)
+            nc.vector.tensor_copy(out=swapped[:, :, 0, :], in_=plain[:, :, 1, :])
+            nc.vector.tensor_scalar(
+                out=swapped[:, :, 1, :], in0=plain[:, :, 0, :], scalar1=-1.0, scalar2=None, op0=ALU.mult
+            )
 
-        def build_tab(c, two):
-            ts = slice(c * TCH, (c + 1) * TCH)
-            src = cos_sb if two == 0 else sinsw
+        def build_table(chunk, product):
+            tiles = slice(chunk * TAB, (chunk + 1) * TAB)
+            angle = cos_sb if product == 0 else sin_swapped
             nc.gpsimd.tensor_tensor(
-                out=tab[:, ts, :, two, :],
-                in0=src[:, ts, :].unsqueeze(2).to_broadcast([P, TCH, 2, HD]),
-                in1=gains[:].unsqueeze(1).to_broadcast([P, TCH, 2, HD]),
+                out=table[:, tiles, :, product, :],
+                in0=angle[:, tiles, :].unsqueeze(2).to_broadcast([P, TAB, 2, HD]),
+                in1=gains[:].unsqueeze(1).to_broadcast([P, TAB, 2, HD]),
                 op=ALU.mult,
             )
 
-        xts = {}
-        xgs = {}
-        xcodes = {}
+        x_banks = {}
+        x_groups = {}
+        x_codes = {}
 
-        def x_transpose(pr):
-            xw = xc[pr][:].bitcast(F32)
-            xt = ps_t.tile([P, 512], F32, name="xt")
+        def transpose_x(pair):
+            words = x_raw[pair][:].bitcast(F32)
+            bank = psum_t.tile([P, 2, 2, P], F32, name="x_bank")
             for a in range(2):
                 for u in range(2):
-                    nc.tensor.transpose(
-                        xt[:, (a * 2 + u) * P : (a * 2 + u + 1) * P], xw[:, a, u * P : (u + 1) * P], ident[:]
-                    )
-            xts[pr] = xt
+                    nc.tensor.transpose(bank[:, a, u, :], words[:, a, u * P : (u + 1) * P], identity[:])
+            x_banks[pair] = bank
 
-        def x_copy(pr, eng_copy):
-            xg = xgp.tile([P, 2, P, 4], BF16, name="xg", align_bytes=64)
-            xgw = xg[:].rearrange("p a k t -> p a (k t)").bitcast(F32).rearrange("p a (k u) -> p a k u", u=2)
-            eng_copy(out=xgw, in_=xts[pr][:].rearrange("p (a u k) -> p a k u", a=2, u=2))
-            xgs[pr] = xg
+        def copy_x(pair, copy):
+            grouped = x_grouped.tile([P, 2, P, PACK], BF16, name="x_group", align_bytes=64)
+            as_words = grouped[:].rearrange("p a n t -> p a (n t)").bitcast(F32).rearrange("p a (n u) -> p a n u", u=2)
+            copy(out=as_words, in_=x_banks[pair][:].rearrange("p a u n -> p a n u"))
+            x_groups[pair] = grouped
 
-        def x_quant(pr):
-            xcod = xq.tile([P, 2 * P], U32, name="xcod", align_bytes=64)
-            xsc = xq.tile([P, 2 * P], U8, name="xsc", align_bytes=64)
+        def quantise_x(pair):
+            codes = x_mx.tile([P, 2 * P], U32, name="x_code", align_bytes=64)
+            scales = x_mx.tile([P, 2 * P], U8, name="x_scale", align_bytes=64)
             nc.vector.quantize_mx(
-                out=xcod[:].bitcast(FP8X4), scales=xsc[:], in_=xgs[pr][:].rearrange("p a k t -> p (a k t)")
+                out=codes[:].bitcast(FP8X4), scales=scales[:], in_=x_groups[pair][:].rearrange("p a n t -> p (a n t)")
             )
-            xcodes[pr] = (xcod, xsc)
+            x_codes[pair] = (codes, scales)
 
-        x_transpose(0)
-        x_copy(0, nc.scalar.copy)
+        def x_copier(pair):
+            return nc.scalar.copy if pair % 2 == 0 else nc.vector.tensor_copy
+
+        pair_behind_tile = {max(2 * pair - 3, 0): pair for pair in range(1, NPAIR)}
+
+        transpose_x(0)
+        copy_x(0, x_copier(0))
         regroup_w(0, nc.vector.tensor_copy)
         regroup_w(1, nc.scalar.copy)
-        x_quant(0)
-        quant_w(0)
+        quantise_x(0)
+        quantise_w(0)
         regroup_w(2, nc.vector.tensor_copy)
-        quant_w(1)
-        quant_w(2)
-        swap_sin(0, TCH)
+        quantise_w(1)
+        quantise_w(2)
+        swap_sin(0, TAB)
 
-        accs = {}
+        products = {}
         sums = {}
-        rstds = {}
+        factors = {}
 
-        def factors(t):
-            rstd = small.tile([P, 3 * H], F32, name="rstd")
+        def take_factors(t):
+            factor = small.tile([P, 3 * H], F32, name="factor")
             nc.scalar.activation(
-                out=rstd[:], in_=sums[t][:], func=ACT.Abs_reciprocal_sqrt, bias=eps_t[:, 0:1], scale=1.0 / HD
+                out=factor[:], in_=sums[t][:], func=ACT.Abs_reciprocal_sqrt, bias=eps_tile[:, 0:1], scale=1.0 / HD
             )
-            rstds[t] = rstd
+            factors[t] = factor
 
         def finish(t):
-            c, a = divmod(t, TCH)
-            acc = accs[t]
-            rstd = rstds[t]
-            if t % 2 == 1 and (t + 3) // 2 < NP:
-                x_copy((t + 3) // 2, nc.vector.tensor_copy)
-            if t % 2 == 0 and t >= 2 and (t + 2) // 2 < NP:
-                x_quant((t + 2) // 2)
-            uw = work.tile([P, 2, 2, H * HD], F32, name="uw")
+            chunk, in_chunk = divmod(t, TAB)
+            y = products[t]
+            factor = factors[t]
+            pair = pair_behind_tile.get(t)
+            if pair is not None and pair % 2 == 1 and t > 0:
+                copy_x(pair, x_copier(pair))
+            if t % 2 == 0 and t >= 2 and t // 2 + 1 < NPAIR:
+                quantise_x(t // 2 + 1)
+            both = work.tile([P, 2, 2, H * HD], F32, name="both")
             for k in range(2):
                 for h in range(H):
                     nc.vector.scalar_tensor_tensor(
-                        out=uw[:, k, :, h * HD : (h + 1) * HD],
-                        in0=acc[k][:, h : h + 1, :].to_broadcast([P, 2, HD]),
-                        scalar=rstd[:, k * H + h : k * H + h + 1],
-                        in1=tab[:, t, k, :, :],
+                        out=both[:, k, :, h * HD : (h + 1) * HD],
+                        in0=y[k][:, h : h + 1, :].to_broadcast([P, 2, HD]),
+                        scalar=factor[:, k * H + h : k * H + h + 1],
+                        in1=table[:, t, k, :, :],
                         op0=ALU.mult,
                         op1=ALU.mult,
                     )
-            ov = work.tile([P, H, HD], F32, name="ov")
+            v_out = work.tile([P, H, HD], F32, name="v_out")
             nc.vector.tensor_tensor(
-                out=ov[:],
-                in0=acc[2][:],
-                in1=rstd[:, 2 * H : 3 * H].unsqueeze(2).to_broadcast([P, H, HD]),
+                out=v_out[:],
+                in0=y[2][:],
+                in1=factor[:, 2 * H : 3 * H].unsqueeze(2).to_broadcast([P, H, HD]),
                 op=ALU.mult,
             )
-            if a < 2 and c + 2 < NTC:
-                build_tab(c + 2, a)
-            o = work.tile([P, 2, H * HD], F32, name="o")
-            ovw = o[:].rearrange("p k (m s i) -> p k m s i", s=2, i=16)
-            uv = uw[:].rearrange("p k two (m s i) -> p k two m s i", s=2, i=16)
+            if in_chunk < 2 and chunk + 2 < NTAB:
+                build_table(chunk + 2, in_chunk)
+            qk_out = work.tile([P, 2, H * HD], F32, name="qk_out")
+            out_halves = qk_out[:].rearrange("p k (m s i) -> p k m s i", s=2, i=16)
+            halves = both[:].rearrange("p k two (m s i) -> p k two m s i", s=2, i=16)
             adder = nc.vector if t == NT - 1 else nc.gpsimd
             for s in range(2):
                 adder.tensor_tensor(
-                    out=ovw[:, :, :, s, :], in0=uv[:, :, 0, :, s, :], in1=uv[:, :, 1, :, 1 - s, :], op=ALU.add
+                    out=out_halves[:, :, :, s, :],
+                    in0=halves[:, :, 0, :, s, :],
+                    in1=halves[:, :, 1, :, 1 - s, :],
+                    op=ALU.add,
                 )
-            nc.sync.dma_start(out=out_v[2][:, t, :], in_=ov[:].rearrange("p h f -> p (h f)"))
-            nc.sync.dma_start(out=out_v[0][:, t, :], in_=o[:, 0, :])
-            nc.sync.dma_start(out=out_v[1][:, t, :], in_=o[:, 1, :])
+            nc.sync.dma_start(out=out_views[2][:, t, :], in_=v_out[:].rearrange("p h f -> p (h f)"))
+            nc.sync.dma_start(out=out_views[0][:, t, :], in_=qk_out[:, 0, :])
+            nc.sync.dma_start(out=out_views[1][:, t, :], in_=qk_out[:, 1, :])
 
         for t in range(NT):
-            pr, a = divmod(t, 2)
-            xcod, xsc = xcodes[pr]
-            acc = []
+            codes, scales = x_codes[t // 2]
+            tokens = slice((t % 2) * P, (t % 2 + 1) * P)
+            y = []
             for i in range(3):
-                b = ps_m.tile([P, H, HD], F32, name="acc")
+                bank = psum_y.tile([P, H, HD], F32, name="y_bank")
                 nc.tensor.matmul_mx(
-                    out=b[:].rearrange("p h f -> p (h f)"),
-                    lhsT=xcod[:, a * P : (a + 1) * P].bitcast(FP8X4),
-                    lhsT_scale=xsc[:, a * P : (a + 1) * P],
-                    rhs=wc[:, i * 512 : (i + 1) * 512].bitcast(FP8X4),
-                    rhs_scale=ws[:, i * 512 : (i + 1) * 512],
+                    out=bank[:].rearrange("p h f -> p (h f)"),
+                    lhsT=codes[:, tokens].bitcast(FP8X4),
+                    lhsT_scale=scales[:, tokens],
+                    rhs=w_codes[:, i * D : (i + 1) * D].bitcast(FP8X4),
+                    rhs_scale=w_scales[:, i * D : (i + 1) * D],
                     start=True,
                     stop=True,
                 )
-                acc.append(b)
-            accs[t] = acc
+                y.append(bank)
+            products[t] = y
+            pair = pair_behind_tile.get(t)
+            if pair is not None:
+                transpose_x(pair)
             if t == 0:
-                x_transpose(1)
-                x_copy(1, nc.vector.tensor_copy)
-                swap_sin(TCH, NT)
-                x_quant(1)
-                for c in range(2):
-                    for two in range(2):
-                        build_tab(c, two)
-            if a == 1 and (t + 3) // 2 < NP:
-                x_transpose((t + 3) // 2)
+                copy_x(1, x_copier(1))
+                swap_sin(TAB, NT)
+                quantise_x(1)
+                for chunk in range(2):
+                    for product in range(2):
+                        build_table(chunk, product)
 
-            ss = small.tile([P, 3 * H], F32, name="ss")
-            sums[t] = ss
+            squares = small.tile([P, 3 * H], F32, name="squares")
+            sums[t] = squares
             for j in range(3 * H):
-                junk = small.tile([P, HD], BF16, name="junk")
+                unused = small.tile([P, HD], BF16, name="unused")
                 nc.scalar.activation(
-                    out=junk[:], in_=acc[j // H][:, j % H, :], func=ACT.Square, accum_out=ss[:, j : j + 1]
+                    out=unused[:], in_=y[j // H][:, j % H, :], func=ACT.Square, accum_out=squares[:, j : j + 1]
                 )
                 if j == LAG - 1 and t > 0:
-                    factors(t - 1)
+                    take_factors(t - 1)
+            if pair is not None and pair % 2 == 0:
+                copy_x(pair, x_copier(pair))
             if t > 0:
                 finish(t - 1)
-        factors(NT - 1)
+        take_factors(NT - 1)
         finish(NT - 1)

from contextlib import ExitStack

import concourse.mybir as mybir
from concourse.masks import make_identity

F32 = mybir.dt.float32
BF16 = mybir.dt.bfloat16
U32 = mybir.dt.uint32
U8 = mybir.dt.uint8
FP8X4 = mybir.dt.float8_e4m3fn_x4
ALU = mybir.AluOpType
ACT = mybir.ActivationFunctionType

N, D, H, HD = 4096, 512, 8, 64
P = 128
PACK = 4
NT = N // P
NPAIR = NT // 2
TAB = 4
NTAB = NT // TAB
LAG = 4
RING = 7
EPS = 1e-6
FLOPS = 2 * N * D * 3 * H * HD


def tile_torchgemma4visionattention_pa_t_kernel(
    tc, hidden_states, cos, sin, Wq, Wk, Wv, q_scale, k_scale, out_0, out_1, out_2
):
    nc = tc.nc
    with ExitStack() as ctx:
        ctx.enter_context(tc.manual_schedule())
        const = ctx.enter_context(tc.tile_pool(name="const", bufs=1))
        x_in = ctx.enter_context(tc.tile_pool(name="x_in", bufs=NPAIR))
        x_grouped = ctx.enter_context(tc.tile_pool(name="x_grouped", bufs=2))
        x_mx = ctx.enter_context(tc.tile_pool(name="x_mx", bufs=4))
        small = ctx.enter_context(tc.tile_pool(name="small", bufs=4))
        work = ctx.enter_context(tc.tile_pool(name="work", bufs=4))
        psum_t = ctx.enter_context(tc.psum_pool(name="psum_t", bufs=1))
        psum_y = ctx.enter_context(tc.psum_pool(name="psum_y", bufs=RING))

        x_view = hidden_states.rearrange("(p t) d -> p t d", t=NT)
        cos_view = cos.rearrange("(p t) f -> p t f", t=NT)
        sin_view = sin.rearrange("(p t) f -> p t f", t=NT)
        out_views = [o.rearrange("(p t) h f -> p t (h f)", t=NT) for o in (out_0, out_1, out_2)]

        w_raw = []
        x_raw = []

        def load_w(w, label):
            raw = const.tile([P, PACK, D], BF16, name="w_raw_" + label)
            nc.sync.dma_start(
                out=raw[:].rearrange("p (u e) c -> p u e c", u=2),
                in_=w.rearrange("(u p e) c -> p u e c", u=2, e=2),
            )
            w_raw.append(raw)

        def load_x(pair):
            raw = x_in.tile([P, 2, D], BF16, name="x_raw")
            nc.sync.dma_start(out=raw[:], in_=x_view[:, 2 * pair : 2 * pair + 2, :])
            x_raw.append(raw)

        gains = const.tile([P, 2, HD], BF16, name="gains")
        cos_sb = const.tile([P, NT, HD], BF16, name="cos_sb")
        sin_sb = const.tile([P, NT, HD], BF16, name="sin_sb")
        load_x(0)
        load_w(Wq, "q")
        load_w(Wk, "k")
        load_w(Wv, "v")
        nc.sync.dma_start(out=gains[:, 0, :], in_=q_scale.partition_broadcast(P))
        nc.sync.dma_start(out=gains[:, 1, :], in_=k_scale.partition_broadcast(P))
        nc.sync.dma_start(out=cos_sb[:, 0:TAB, :], in_=cos_view[:, 0:TAB, :])
        nc.sync.dma_start(out=sin_sb[:, 0:TAB, :], in_=sin_view[:, 0:TAB, :])
        load_x(1)
        nc.sync.dma_start(out=sin_sb[:, TAB:NT, :], in_=sin_view[:, TAB:NT, :])
        nc.sync.dma_start(out=cos_sb[:, TAB:NT, :], in_=cos_view[:, TAB:NT, :])
        for pair in range(2, NPAIR):
            load_x(pair)

        identity = const.tile([P, P], F32, name="identity")
        make_identity(nc, identity[:])
        eps_tile = const.tile([P, 1], F32, name="eps_tile")
        nc.vector.memset(eps_tile[:], EPS)
        warm = const.tile([P, 1], F32, name="warm")
        nc.scalar.activation(out=warm[:], in_=eps_tile[:], func=ACT.Abs_reciprocal_sqrt)

        w_codes = const.tile([P, 3 * D], U32, name="w_codes", align_bytes=64)
        w_scales = const.tile([P, 3 * D], U8, name="w_scales", align_bytes=64)
        w_grouped = [const.tile([P, D, PACK], BF16, name="w_grouped%d" % i, align_bytes=64) for i in range(3)]

        def regroup_w(i, copy):
            copy(
                out=w_grouped[i][:].rearrange("p (c i) t -> p c t i", i=4),
                in_=w_raw[i][:].rearrange("p t (c i) -> p c t i", i=4),
            )

        def quantise_w(i):
            nc.vector.quantize_mx(
                out=w_codes[:, i * D : (i + 1) * D].bitcast(FP8X4),
                scales=w_scales[:, i * D : (i + 1) * D],
                in_=w_grouped[i][:].rearrange("p c t -> p (c t)"),
            )

        sin_swapped = const.tile([P, NT, HD], BF16, name="sin_swapped")
        table = const.tile([P, NT, 2, 2, HD], F32, name="table")

        def swap_sin(t0, t1):
            plain = sin_sb[:, t0:t1, :].rearrange("p t (b s i) -> p (t b) s i", b=2, s=2)
            swapped = sin_swapped[:, t0:t1, :].rearrange("p t (b s i) -> p (t b) s i", b=2, s=2)
            nc.vector.tensor_copy(out=swapped[:, :, 0, :], in_=plain[:, :, 1, :])
            nc.vector.tensor_scalar(
                out=swapped[:, :, 1, :], in0=plain[:, :, 0, :], scalar1=-1.0, scalar2=None, op0=ALU.mult
            )

        def build_table(chunk, product):
            tiles = slice(chunk * TAB, (chunk + 1) * TAB)
            angle = cos_sb if product == 0 else sin_swapped
            nc.gpsimd.tensor_tensor(
                out=table[:, tiles, :, product, :],
                in0=angle[:, tiles, :].unsqueeze(2).to_broadcast([P, TAB, 2, HD]),
                in1=gains[:].unsqueeze(1).to_broadcast([P, TAB, 2, HD]),
                op=ALU.mult,
            )

        x_banks = {}
        x_groups = {}
        x_codes = {}

        def transpose_x(pair):
            words = x_raw[pair][:].bitcast(F32)
            bank = psum_t.tile([P, 2, 2, P], F32, name="x_bank")
            for a in range(2):
                for u in range(2):
                    nc.tensor.transpose(bank[:, a, u, :], words[:, a, u * P : (u + 1) * P], identity[:])
            x_banks[pair] = bank

        def copy_x(pair, copy):
            grouped = x_grouped.tile([P, 2, P, PACK], BF16, name="x_group", align_bytes=64)
            as_words = grouped[:].rearrange("p a n t -> p a (n t)").bitcast(F32).rearrange("p a (n u) -> p a n u", u=2)
            copy(out=as_words, in_=x_banks[pair][:].rearrange("p a u n -> p a n u"))
            x_groups[pair] = grouped

        def quantise_x(pair):
            codes = x_mx.tile([P, 2 * P], U32, name="x_code", align_bytes=64)
            scales = x_mx.tile([P, 2 * P], U8, name="x_scale", align_bytes=64)
            nc.vector.quantize_mx(
                out=codes[:].bitcast(FP8X4), scales=scales[:], in_=x_groups[pair][:].rearrange("p a n t -> p (a n t)")
            )
            x_codes[pair] = (codes, scales)

        def x_copier(pair):
            return nc.scalar.copy if pair % 2 == 0 else nc.vector.tensor_copy

        pair_behind_tile = {max(2 * pair - 3, 0): pair for pair in range(1, NPAIR)}

        transpose_x(0)
        copy_x(0, x_copier(0))
        regroup_w(0, nc.vector.tensor_copy)
        regroup_w(1, nc.scalar.copy)
        quantise_x(0)
        quantise_w(0)
        regroup_w(2, nc.vector.tensor_copy)
        quantise_w(1)
        quantise_w(2)
        swap_sin(0, TAB)

        products = {}
        sums = {}
        factors = {}

        def take_factors(t):
            factor = small.tile([P, 3 * H], F32, name="factor")
            nc.scalar.activation(
                out=factor[:], in_=sums[t][:], func=ACT.Abs_reciprocal_sqrt, bias=eps_tile[:, 0:1], scale=1.0 / HD
            )
            factors[t] = factor

        def finish(t):
            chunk, in_chunk = divmod(t, TAB)
            y = products[t]
            factor = factors[t]
            pair = pair_behind_tile.get(t)
            if pair is not None and pair % 2 == 1 and t > 0:
                copy_x(pair, x_copier(pair))
            if t % 2 == 0 and t >= 2 and t // 2 + 1 < NPAIR:
                quantise_x(t // 2 + 1)
            both = work.tile([P, 2, 2, H * HD], F32, name="both")
            for k in range(2):
                for h in range(H):
                    nc.vector.scalar_tensor_tensor(
                        out=both[:, k, :, h * HD : (h + 1) * HD],
                        in0=y[k][:, h : h + 1, :].to_broadcast([P, 2, HD]),
                        scalar=factor[:, k * H + h : k * H + h + 1],
                        in1=table[:, t, k, :, :],
                        op0=ALU.mult,
                        op1=ALU.mult,
                    )
            v_out = work.tile([P, H, HD], F32, name="v_out")
            nc.vector.tensor_tensor(
                out=v_out[:],
                in0=y[2][:],
                in1=factor[:, 2 * H : 3 * H].unsqueeze(2).to_broadcast([P, H, HD]),
                op=ALU.mult,
            )
            if in_chunk < 2 and chunk + 2 < NTAB:
                build_table(chunk + 2, in_chunk)
            qk_out = work.tile([P, 2, H * HD], F32, name="qk_out")
            out_halves = qk_out[:].rearrange("p k (m s i) -> p k m s i", s=2, i=16)
            halves = both[:].rearrange("p k two (m s i) -> p k two m s i", s=2, i=16)
            adder = nc.vector if t == NT - 1 else nc.gpsimd
            for s in range(2):
                adder.tensor_tensor(
                    out=out_halves[:, :, :, s, :],
                    in0=halves[:, :, 0, :, s, :],
                    in1=halves[:, :, 1, :, 1 - s, :],
                    op=ALU.add,
                )
            nc.sync.dma_start(out=out_views[2][:, t, :], in_=v_out[:].rearrange("p h f -> p (h f)"))
            nc.sync.dma_start(out=out_views[0][:, t, :], in_=qk_out[:, 0, :])
            nc.sync.dma_start(out=out_views[1][:, t, :], in_=qk_out[:, 1, :])

        for t in range(NT):
            codes, scales = x_codes[t // 2]
            tokens = slice((t % 2) * P, (t % 2 + 1) * P)
            y = []
            for i in range(3):
                bank = psum_y.tile([P, H, HD], F32, name="y_bank")
                nc.tensor.matmul_mx(
                    out=bank[:].rearrange("p h f -> p (h f)"),
                    lhsT=codes[:, tokens].bitcast(FP8X4),
                    lhsT_scale=scales[:, tokens],
                    rhs=w_codes[:, i * D : (i + 1) * D].bitcast(FP8X4),
                    rhs_scale=w_scales[:, i * D : (i + 1) * D],
                    start=True,
                    stop=True,
                )
                y.append(bank)
            products[t] = y
            pair = pair_behind_tile.get(t)
            if pair is not None:
                transpose_x(pair)
            if t == 0:
                copy_x(1, x_copier(1))
                swap_sin(TAB, NT)
                quantise_x(1)
                for chunk in range(2):
                    for product in range(2):
                        build_table(chunk, product)

            squares = small.tile([P, 3 * H], F32, name="squares")
            sums[t] = squares
            for j in range(3 * H):
                unused = small.tile([P, HD], BF16, name="unused")
                nc.scalar.activation(
                    out=unused[:], in_=y[j // H][:, j % H, :], func=ACT.Square, accum_out=squares[:, j : j + 1]
                )
                if j == LAG - 1 and t > 0:
                    take_factors(t - 1)
            if pair is not None and pair % 2 == 0:
                copy_x(pair, x_copier(pair))
            if t > 0:
                finish(t - 1)
        take_factors(NT - 1)
        finish(NT - 1)
